import numpy as np
import ml_dtypes


def mxq(x, axis, fmt="e4m3"):
    dtype, down = {"e4m3": (ml_dtypes.float8_e4m3fn, 7), "e5m2": (ml_dtypes.float8_e5m2, 14)}[fmt]
    v = np.moveaxis(np.asarray(x, np.float32).astype(ml_dtypes.bfloat16).astype(np.float64), axis, -1)
    blocks = v.reshape(v.shape[:-1] + (-1, 32))
    amax = np.abs(blocks).max(-1, keepdims=True)
    byte = np.maximum(np.where(amax > 0, np.frexp(amax)[1] - 1 + 127, 0) - down, 1)
    scale = np.exp2(byte - 127.0)
    codes = (blocks / scale).astype(np.float32).astype(dtype).astype(np.float64)
    return np.moveaxis((codes * scale).reshape(v.shape), -1, axis)


WIDE = False


def mx_kscale(k):
    if not WIDE:
        return np.ones(k)
    levels = np.array([18, -18])
    if k % 512:
        return np.exp2(np.random.permutation(np.resize(levels, k // 32))).repeat(32)
    a = np.empty((k // 512, 16))
    for p in range(k // 512):
        a[p, :8] = np.random.permutation(np.resize(levels, 8))
        for g in range(8):
            far = levels[np.abs(levels - a[p, g]) >= 10]
            a[p, g + 8] = far[np.random.randint(len(far))]
    return np.exp2(a.ravel()).repeat(32)


BF16 = ml_dtypes.bfloat16


def bf(x):
    return np.asarray(x, np.float32).astype(BF16)


def f64(x):
    return np.asarray(x).astype(np.float64)


B, C, W, H, O = 1024, 32, 8, 8, 1024
K = C * W * H
G = np.sqrt(W * H)
SLO, SHI = 1.0 + 0.03 * G, 2.0 + 0.25 * G


def gaussians(cx, cy, sigma):
    grid_x = np.linspace(-(W - 1) / 2.0, (W - 1) / 2.0, W).reshape(1, 1, W, 1)
    grid_y = np.linspace(-(H - 1) / 2.0, (H - 1) / 2.0, H).reshape(1, 1, 1, H)
    d = (cx - grid_x) ** 2 + (cy - grid_y) ** 2
    return np.exp(-d / sigma ** 2)


def setup_inputs():
    s = mx_kscale(B)
    u = mx_kscale(O)
    return {"x": bf(np.random.standard_normal((B, C, W, H)) * s.reshape(B, 1, 1, 1)),
            "cx": bf(np.random.uniform(-W / 2.0, W / 2.0, (O, 1, 1, 1))),
            "cy": bf(np.random.uniform(-H / 2.0, H / 2.0, (O, 1, 1, 1))),
            "sigma": bf(np.random.uniform(SLO, SHI, (O, 1, 1, 1))),
            "features": bf(np.random.standard_normal((O, C, 1, 1)) * 2.0 / (np.sqrt(C) * (SLO + SHI)) / u.reshape(O, 1, 1, 1)),
            "bias": bf(np.random.standard_normal(O)),
            "grad_out": bf(np.random.standard_normal((B, O)) * np.exp2(np.random.randint(-6, 1, (B, 1))) / s[:, None] * u)}


def reference(x, cx, cy, sigma, features, bias, grad_out):
    xf = f64(x).reshape(B, K)
    g = f64(grad_out)
    spatial = gaussians(f64(cx), f64(cy), f64(sigma))
    weight = (spatial * f64(features)).reshape(O, K)
    dx = mxq(g, 1, "e5m2") @ mxq(weight, 0, "e4m3")
    dweight = mxq(g, 0, "e5m2").T @ mxq(xf, 0, "e4m3")
    dfeatures = (dweight.reshape(O, C, W, H) * spatial).sum(axis=(2, 3)).reshape(O, C, 1, 1)
    return dx.reshape(B, C, W, H), dfeatures

@@ -1,0 +1,314 @@
+from contextlib import ExitStack
+
+import concourse.mybir as mybir
+from concourse.masks import make_identity
+
+B, C, W, H, O = 1024, 32, 8, 8, 1024
+S = W * H
+K = C * S
+FLOPS = 2 * 2 * B * O * K
+BYTES = 2 * (B * K + B * O + O * C + 3 * O) + 4 * (B * K + O * C)
+
+F32 = mybir.dt.float32
+BF16 = mybir.dt.bfloat16
+U32 = mybir.dt.uint32
+U8 = mybir.dt.uint8
+E4 = mybir.dt.float8_e4m3fn_x4
+E5 = mybir.dt.float8_e5m2_x4
+ALU = mybir.AluOpType
+ACT = mybir.ActivationFunctionType
+P = 128
+
+WE = 'VVVGVGGG'
+IXE = ['VVVV', 'SSSS', 'SSSS', 'SSSG']
+E1S = 0
+E2G = 1
+WARM = 8
+WARM0 = 2
+OUTB = 8
+WB = {'V': 4, 'G': 1}
+XB = [4, 4, 4, 4]
+L3 = 2
+RL = 3
+QX = 5
+PRE = []
+
+
+def tile_gaussianspatialxfeaturelinear_v_kernel(tc, x, cx, cy, sigma, features, bias, grad_out, out_0, out_1):
+    nc = tc.nc
+    xf = x.rearrange("b c i j -> b (c i j)")
+    dxf = out_0.rearrange("(g p j) c i k -> g j p (c i k)", p=P, j=4)
+    with ExitStack() as ctx:
+        keep = ctx.enter_context(tc.tile_pool(name="keep", bufs=1))
+        stage = ctx.enter_context(tc.tile_pool(name="stage", bufs=2))
+        outp = ctx.enter_context(tc.tile_pool(name="outp", bufs=OUTB))
+        fpsum = ctx.enter_context(tc.psum_pool(name="fpsum", bufs=1))
+        psum = ctx.enter_context(tc.psum_pool(name="psum", bufs=7))
+        ctx.enter_context(tc.manual_schedule())
+
+        cen = [keep.tile([P, 2, 4], BF16, name="cen%d" % a) for a in range(2)]
+        sg = keep.tile([P, 8], BF16, name="sg")
+        f_raw = keep.tile([P, 2, 4, C], BF16, name="f_raw")
+        g_raw = [keep.tile([P, 4 * O], BF16, name="g_raw%d" % g, align_bytes=64) for g in range(2)]
+        x_raw = [keep.tile([P, 4 * K], BF16, name="x_raw%d" % g, align_bytes=64) for g in range(2)]
+        for a, src in enumerate((cx, cy)):
+            nc.sync.dma_start(out=cen[a][:], in_=src.rearrange("(h p t) a b c -> p h (t a b c)", p=P, t=4))
+        nc.sync.dma_start(out=sg[:].rearrange("p (h t) -> p h t", t=4), in_=sigma.rearrange("(h p t) a b c -> p h (t a b c)", p=P, t=4))
+        nc.sync.dma_start(out=f_raw[:].rearrange("p h t c -> p h (t c)"), in_=features.rearrange("(h p t) c a b -> p h (t c a b)", p=P, t=4))
+        for g in range(2):
+            nc.sync.dma_start(out=g_raw[g][:], in_=grad_out[512 * g:512 * (g + 1), :].rearrange("(p j) o -> p (j o)", j=4))
+        for g in range(2):
+            nc.sync.dma_start(out=x_raw[g][:], in_=xf[512 * g:512 * (g + 1), :].rearrange("(p j) k -> p (j k)", j=4))
+
+        grid = keep.tile([P, W], F32, name="grid")
+        nc.gpsimd.iota(grid[:], [[1, W]], base=0, channel_multiplier=0, allow_small_or_imprecise_dtypes=True)
+        id16 = keep.tile([P, P], BF16, name="id16")
+        make_identity(nc, id16[:])
+        id32 = keep.tile([P, P], F32, name="id32")
+        make_identity(nc, id32[:])
+        scratch = keep.tile([P, W], F32, name="scratch")
+        nc.scalar.activation(out=scratch[:], in_=grid[:], func=ACT.Exp, scale=-1.0)
+        gridc = keep.tile([P, W], F32, name="gridc")
+        nc.vector.tensor_scalar(out=gridc[:], in0=grid[:], scalar1=-(W - 1) / 2.0, scalar2=None, op0=ALU.add)
+        if WARM:
+            wsrc = keep.tile([P, 512], BF16, name="wsrc")
+            nc.vector.memset(wsrc[:], 0.0)
+            wb = psum.tile([P, 512], F32, name="warm", tag="bank")
+            for rep in range(WARM0):
+                nc.tensor.matmul(wb[:], lhsT=id16[:], rhs=wsrc[:], start=True, stop=True)
+
+        s2 = keep.tile([P, 2, 8], F32, name="s2")
+        sgb = sg[:].unsqueeze(1).to_broadcast([P, 2, 8])
+        nc.vector.tensor_tensor(out=s2[:], in0=sgb, in1=sgb, op=ALU.mult)
+        d = keep.tile([P, 2, 2, W, 4], F32, name="d")
+        for a in range(2):
+            nc.vector.tensor_tensor(out=d[:, a], in0=cen[a][:].unsqueeze(2).to_broadcast([P, 2, W, 4]),
+                                    in1=gridc[:].unsqueeze(1).unsqueeze(3).to_broadcast([P, 2, W, 4]), op=ALU.subtract)
+        r2 = keep.tile([P, 16], F32, name="r2")
+        nc.vector.reciprocal(out=r2[:], in_=s2[:].rearrange("p a q -> p (a q)"))
+        d2 = keep.tile([P, 4, W, 4], F32, name="d2")
+        dv = d[:].rearrange("p a h i t -> p (a h) i t")
+        nc.vector.tensor_tensor(out=d2[:], in0=dv, in1=dv, op=ALU.mult)
+        arg = keep.tile([P, 4, W, 4], F32, name="arg")
+        nc.vector.tensor_tensor(out=arg[:], in0=d2[:], in1=r2[:].rearrange("p (q t) -> p q t", t=4).unsqueeze(2).to_broadcast([P, 4, W, 4]), op=ALU.mult)
+        e = keep.tile([P, 2, 2, W, 4], F32, name="e")
+        nc.scalar.activation(out=e[:].rearrange("p a h i t -> p (a h i t)"), in_=arg[:].rearrange("p q i t -> p (q i t)"), func=ACT.Exp, scale=-1.0)
+
+        f_ps = fpsum.tile([P, 2, C, 4], F32, name="f_ps")
+        nc.tensor.matmul(f_ps[:].rearrange("p h c t -> p (h c t)"), lhsT=id16[:], rhs=f_raw[:].rearrange("p h t c -> p h c t"), start=True, stop=True)
+        for rep in range(WARM - WARM0):
+            nc.tensor.matmul(wb[:], lhsT=id16[:], rhs=wsrc[:], start=True, stop=True)
+        f_sb = keep.tile([P, 2, C, 4], F32, name="f_sb")
+        nc.scalar.copy(out=f_sb[:], in_=f_ps[:])
+        sp = keep.tile([P, 2, W, H, 4], F32, name="sp")
+        for h in range(2):
+            nc.vector.tensor_tensor(out=sp[:, h], in0=e[:, 0, h].unsqueeze(2).to_broadcast([P, W, H, 4]),
+                                    in1=e[:, 1, h].unsqueeze(1).to_broadcast([P, W, H, 4]), op=ALU.mult)
+        ey = keep.tile([P, 2, 4, H], F32, name="ey")
+
+        gt_bf = keep.tile([P, 8, 1024], BF16, name="gt_bf", align_bytes=64)
+        gt_c = keep.tile([P, 8, 2, P], U32, name="gt_c", align_bytes=64)
+        gt_s = keep.tile([P, 8, 2, P], U8, name="gt_s", align_bytes=64)
+        gi_bf = [keep.tile([P, 4 * O], BF16, name="gi_bf%d" % g, align_bytes=64) for g in range(2)]
+        gi_c = keep.tile([P, 2, O], U32, name="gi_c", align_bytes=64)
+        gi_s = keep.tile([P, 2, O], U8, name="gi_s", align_bytes=64)
+        w_c = [keep.tile([P, 2, 512], U32, name="w_c%d" % n, align_bytes=64) for n in range(4)]
+        w_s = [keep.tile([P, 2, 512], U8, name="w_s%d" % n, align_bytes=64) for n in range(4)]
+        x_c = [keep.tile([P, 2, 512], U32, name="x_c%d" % n, align_bytes=64) for n in range(4)]
+        x_s = [keep.tile([P, 2, 512], U8, name="x_s%d" % n, align_bytes=64) for n in range(4)]
+        acc = [keep.tile([P, C * H], F32, name="acc%d" % q) for q in range(8)]
+        df = keep.tile([P, 2, 4, C], F32, name="df")
+        w_bf = {}
+        x_bf = {}
+        banks = {}
+
+        def transposes(m):
+            g, j = divmod(m, 4)
+            words = g_raw[g][:].bitcast(F32)
+            bank = psum.tile([P, 2, 2, P], F32, name="tr%d" % m, tag="bank")
+            for h in range(2):
+                for u in range(2):
+                    lo = 512 * j + 256 * h
+                    nc.tensor.transpose(bank[:, h, u, :], words[:, lo + u:lo + 256:2], id32[:])
+            nc.scalar.copy(out=gt_bf[:, m, :].bitcast(F32).rearrange("p (h r u) -> p h r u", h=2, u=2),
+                           in_=bank[:].rearrange("p h u r -> p h r u"))
+
+        def quant_gt(m0, cnt):
+            nc.vector.quantize_mx(out=gt_c[:, m0:m0 + cnt].rearrange("p m h r -> p (m h r)").bitcast(E5),
+                                  scales=gt_s[:, m0:m0 + cnt].rearrange("p m h r -> p (m h r)"),
+                                  in_=gt_bf[:, m0:m0 + cnt, :].rearrange("p m w -> p (m w)"))
+
+        def inter_g_pe(g, h, tp):
+            bank = psum.tile([P, 2, 512], BF16, name="ig%d%d%d" % (g, h, tp), tag="bank")
+            src = g_raw[g][:].rearrange("p (j h m t) -> p h t m j", j=4, h=2, t=4)
+            for tt in range(2):
+                nc.tensor.matmul(bank[:, tt, :], lhsT=id16[:], rhs=src[:, h, 2 * tp + tt], start=True, stop=True)
+            lo = 2048 * h + 1024 * tp
+            nc.scalar.copy(out=gi_bf[g][:, lo:lo + 1024], in_=bank[:].rearrange("p a b -> p (a b)"))
+
+        def inter_g(g, h, eng):
+            src = g_raw[g][:].rearrange("p (j h mp m t) -> p h mp t m j", j=4, h=2, m=2, t=4)[:, h]
+            dst = gi_bf[g][:].rearrange("p (h t mp m j) -> p h mp t m j", j=4, h=2, m=2, t=4)[:, h]
+            if eng == 'S':
+                nc.scalar.copy(out=dst, in_=src)
+            else:
+                nc.vector.tensor_copy(out=dst, in_=src)
+
+        def quant_gi(g):
+            nc.vector.quantize_mx(out=gi_c[:, g, :].bitcast(E5), scales=gi_s[:, g, :], in_=gi_bf[g][:])
+
+        def build_w(n, h, c0, c1, eng):
+            if (n, h) not in w_bf:
+                w_bf[n, h] = stage.tile([P, 8, S, 4], BF16, name="w_bf%d%d" % (n, h), tag="w_bf" + eng, bufs=WB[eng], align_bytes=64)
+            if c1 <= c0:
+                return
+            shape = [P, c1 - c0, S, 4]
+            spb = sp[:, h].rearrange("p i j t -> p (i j) t").unsqueeze(1).to_broadcast(shape)
+            src = f_ps if eng == 'V' else f_sb
+            fb = src[:, h, 8 * n + c0:8 * n + c1, :].unsqueeze(2).to_broadcast(shape)
+            (nc.vector if eng == 'V' else nc.gpsimd).tensor_tensor(out=w_bf[n, h][:, c0:c1], in0=fb, in1=spb, op=ALU.mult)
+
+        def quant_w(n, h):
+            nc.vector.quantize_mx(out=w_c[n][:, h, :].bitcast(E4), scales=w_s[n][:, h, :], in_=w_bf[n, h][:].rearrange("p c s t -> p (c s t)"))
+
+        def inter_x(n, g, i0, i1, eng):
+            if (n, g) not in x_bf:
+                x_bf[n, g] = stage.tile([P, 2, C, H, 4], BF16, name="x_bf%d%d" % (n, g), tag="x_bf", bufs=4, align_bytes=64)
+            src = x_raw[g][:].rearrange("p (t c i j) -> p i c j t", t=4, i=W, j=H)[:, 2 * n + i0:2 * n + i1]
+            dst = x_bf[n, g][:, i0:i1]
+            if eng == 'S':
+                nc.scalar.copy(out=dst, in_=src)
+            elif eng == 'V':
+                nc.vector.tensor_copy(out=dst, in_=src)
+            else:
+                nc.gpsimd.tensor_scalar(out=dst, in0=src, scalar1=1.0, scalar2=0.0, op0=ALU.mult, op1=ALU.add)
+
+        def quant_x(n, g):
+            nc.vector.quantize_mx(out=x_c[n][:, g, :].bitcast(E4), scales=x_s[n][:, g, :], in_=x_bf[n, g][:].rearrange("p i c j t -> p (i c j t)"))
+
+        def dx(n, m):
+            bank = psum.tile([P, 512], F32, name="dx%d%d" % (n, m), tag="bank")
+            for h in range(2):
+                nc.tensor.matmul_mx(out=bank[:], lhsT=gt_c[:, m, h, :].bitcast(E5), lhsT_scale=gt_s[:, m, h, :],
+                                    rhs=w_c[n][:, h, :].bitcast(E4), rhs_scale=w_s[n][:, h, :], start=h == 0, stop=h == 1)
+            res = outp.tile([P, 512], F32, name="res%d%d" % (n, m), tag="res")
+            nc.scalar.copy(out=res[:], in_=bank[:])
+            nc.sync.dma_start(out=dxf[m // 4, m % 4, :, 512 * n:512 * (n + 1)], in_=res[:])
+
+        def dw_mm(n, q):
+            bank = psum.tile([P, 512], F32, name="dw%d%d" % (n, q), tag="bank")
+            banks[n, q] = bank
+            cols = slice(P * q, P * (q + 1))
+            for g in range(2):
+                nc.tensor.matmul_mx(out=bank[:], lhsT=gi_c[:, g, cols].bitcast(E5), lhsT_scale=gi_s[:, g, cols],
+                                    rhs=x_c[n][:, g, :].bitcast(E4), rhs_scale=x_s[n][:, g, :], start=g == 0, stop=g == 1)
+
+        def fold(n, q, i2):
+            i = 2 * n + i2
+            part = banks[n, q][:, 256 * i2:256 * (i2 + 1)]
+            ex = e[:, 0, q // 4, i, q % 4:q % 4 + 1]
+            if i == 0:
+                if E1S:
+                    nc.scalar.activation(out=acc[q][:], in_=part, func=ACT.Copy, scale=ex)
+                else:
+                    nc.vector.tensor_scalar(out=acc[q][:], in0=part, scalar1=ex, scalar2=None, op0=ALU.mult)
+            else:
+                nc.vector.scalar_tensor_tensor(out=acc[q][:], in0=part, scalar=ex, in1=acc[q][:], op0=ALU.mult, op1=ALU.add)
+
+        prods = {}
+
+        def fin_mul(q):
+            prods[q] = stage.tile([P, C, H], F32, name="prod%d" % q, tag="prod", bufs=4)
+            (nc.gpsimd if E2G and q < 7 else nc.vector).tensor_tensor(
+                out=prods[q][:], in0=acc[q][:].rearrange("p (c j) -> p c j", j=H),
+                in1=ey[:, q // 4, q % 4, :].unsqueeze(1).to_broadcast([P, C, H]), op=ALU.mult)
+
+        def fin_red(q):
+            nc.vector.tensor_reduce(out=df[:, q // 4, q % 4, :], in_=prods[q][:], axis=mybir.AxisListType.X, op=ALU.add)
+
+        def ig(g, h):
+            for tp in range(2):
+                inter_g_pe(g, h, tp)
+
+        def xi(n, r, engs):
+            if IXE[n][r] in engs:
+                inter_x(n, r // 2, r % 2, r % 2 + 1, IXE[n][r])
+
+        def w(n, h):
+            build_w(n, h, 0, 8, WE[2 * n + h])
+
+        w(1, 1)
+        w(0, 0)
+        w(0, 1)
+        for m in range(4):
+            transposes(m)
+        ig(0, 0)
+        transposes(4)
+        transposes(5)
+        ig(0, 1)
+        transposes(6)
+        transposes(7)
+        quant_w(0, 0)
+        quant_w(0, 1)
+        quant_gt(0, 2)
+        quant_gt(2, 2)
+        quant_w(1, 1)
+        quant_gt(4, 2)
+        quant_gi(0)
+        quant_gt(6, 2)
+        w(1, 0)
+        w(2, 0)
+        w(2, 1)
+        for m in range(4):
+            dx(0, m)
+        ig(1, 0)
+        ig(1, 1)
+        for m in range(4, 8):
+            dx(0, m)
+        quant_w(1, 0)
+        quant_gi(1)
+        for r in range(4):
+            xi(0, r, 'SVG')
+        quant_x(0, 0)
+        quant_x(0, 1)
+        quant_w(2, 0)
+        quant_w(2, 1)
+        todo = [(n, m) for n in range(1, 4) for m in range(8)]
+        for c in range(24 - sum(XB)):
+            dx(*todo.pop(0))
+            if c in PRE:
+                xi(1, PRE.index(c), 'SVG')
+        nc.scalar.copy(out=ey[:], in_=e[:, 1].rearrange("p h j t -> p h t j"))
+        for n in range(4):
+            if n < 2:
+                w(3, n)
+            done = 0
+            for q in range(8):
+                dw_mm(n, q)
+                fold(n, q, 0)
+                if q > 0:
+                    fold(n, q - 1, 1)
+                    if n == 3:
+                        fin_mul(q - 1)
+                if n == 3 and q >= RL:
+                    fin_red(q - RL)
+                if n < 3 and q < 4 and q >= len(PRE):
+                    xi(n + 1, q, 'SVG')
+                if n < 2 and q >= 8 - len(PRE):
+                    xi(n + 2, q - 8 + len(PRE), 'SVG')
+                if n < 3 and q == QX:
+                    quant_x(n + 1, 0)
+                    quant_x(n + 1, 1)
+                    if n < 2:
+                        quant_w(3, n)
+                lim = (XB[n] if n < 3 else L3) * (q + 1) // 8
+                while done < lim:
+                    dx(*todo.pop(0))
+                    done = done + 1
+            fold(n, 7, 1)
+        fin_mul(7)
+        for q in range(8 - RL, 8):
+            fin_red(q)
+        while todo:
+            dx(*todo.pop(0))
+        nc.sync.dma_start(out=out_1.rearrange("(h p t) c a b -> p h (t c a b)", p=P, t=4), in_=df[:].rearrange("p h t c -> p h (t c)"))

@@ -13,302 +13,376 @@ F32 = mybir.dt.float32
 BF16 = mybir.dt.bfloat16
 U32 = mybir.dt.uint32
 U8 = mybir.dt.uint8
-E4 = mybir.dt.float8_e4m3fn_x4
-E5 = mybir.dt.float8_e5m2_x4
+E4M3 = mybir.dt.float8_e4m3fn_x4
+E5M2 = mybir.dt.float8_e5m2_x4
 ALU = mybir.AluOpType
 ACT = mybir.ActivationFunctionType
+
 P = 128
+PACK = 4
+PASS = P * PACK
+PASSES = 2
+N = 512
+COL_TILES = K // N
+ROW_TILES = 8
+TILE_C = C // COL_TILES
+TILE_I = W // COL_TILES
+CJ = C * H
 
-WE = 'VVVGVGGG'
-IXE = ['VVVV', 'SSSS', 'SSSS', 'SSSG']
-E1S = 0
-E2G = 1
-WARM = 8
-WARM0 = 2
-OUTB = 8
-WB = {'V': 4, 'G': 1}
-XB = [4, 4, 4, 4]
-L3 = 2
-RL = 3
-QX = 5
-PRE = []
+GPSIMD_CHANNELS = {(1, 1): 7, (2, 0): 5, (2, 1): TILE_C, (3, 0): TILE_C, (3, 1): TILE_C}
+QUANTISE_AT = 5
+REDUCE_LAG = 2
+WARM_UP = 8
+RESULT_BUFS = 8
+WORK_BANKS = 7
 
 
-def tile_gaussianspatialxfeaturelinear_v_kernel(tc, x, cx, cy, sigma, features, bias, grad_out, out_0, out_1):
+def tile_gaussianspatialxfeaturelinear_v_kernel(
+    tc, x, cx, cy, sigma, features, bias, grad_out, out_0, out_1
+):
     nc = tc.nc
-    xf = x.rearrange("b c i j -> b (c i j)")
-    dxf = out_0.rearrange("(g p j) c i k -> g j p (c i k)", p=P, j=4)
+    x_rows = x.rearrange("b c i j -> b (c i j)")
+    out_0_tiles = out_0.rearrange("(g p r) c i j -> g r p (c i j)", p=P, r=PACK)
+    by_feature = "(h p t) a b c -> p h (t a b c)"
+
     with ExitStack() as ctx:
         keep = ctx.enter_context(tc.tile_pool(name="keep", bufs=1))
-        stage = ctx.enter_context(tc.tile_pool(name="stage", bufs=2))
-        outp = ctx.enter_context(tc.tile_pool(name="outp", bufs=OUTB))
+        stage = ctx.enter_context(tc.tile_pool(name="stage", bufs=1))
         fpsum = ctx.enter_context(tc.psum_pool(name="fpsum", bufs=1))
-        psum = ctx.enter_context(tc.psum_pool(name="psum", bufs=7))
+        psum = ctx.enter_context(tc.psum_pool(name="psum", bufs=WORK_BANKS))
         ctx.enter_context(tc.manual_schedule())
 
-        cen = [keep.tile([P, 2, 4], BF16, name="cen%d" % a) for a in range(2)]
-        sg = keep.tile([P, 8], BF16, name="sg")
-        f_raw = keep.tile([P, 2, 4, C], BF16, name="f_raw")
-        g_raw = [keep.tile([P, 4 * O], BF16, name="g_raw%d" % g, align_bytes=64) for g in range(2)]
-        x_raw = [keep.tile([P, 4 * K], BF16, name="x_raw%d" % g, align_bytes=64) for g in range(2)]
-        for a, src in enumerate((cx, cy)):
-            nc.sync.dma_start(out=cen[a][:], in_=src.rearrange("(h p t) a b c -> p h (t a b c)", p=P, t=4))
-        nc.sync.dma_start(out=sg[:].rearrange("p (h t) -> p h t", t=4), in_=sigma.rearrange("(h p t) a b c -> p h (t a b c)", p=P, t=4))
-        nc.sync.dma_start(out=f_raw[:].rearrange("p h t c -> p h (t c)"), in_=features.rearrange("(h p t) c a b -> p h (t c a b)", p=P, t=4))
-        for g in range(2):
-            nc.sync.dma_start(out=g_raw[g][:], in_=grad_out[512 * g:512 * (g + 1), :].rearrange("(p j) o -> p (j o)", j=4))
-        for g in range(2):
-            nc.sync.dma_start(out=x_raw[g][:], in_=xf[512 * g:512 * (g + 1), :].rearrange("(p j) k -> p (j k)", j=4))
+        centre = [keep.tile([P, PASSES, PACK], BF16, name="centre%d" % a) for a in range(2)]
+        sig = keep.tile([P, PASSES, PACK], BF16, name="sig")
+        f_raw = keep.tile([P, PASSES, PACK, C], BF16, name="f_raw")
+        g_raw = [keep.tile([P, PACK * O], BF16, name="g_raw%d" % g, align_bytes=64) for g in range(PASSES)]
+        x_raw = [keep.tile([P, PACK * K], BF16, name="x_raw%d" % g, align_bytes=64) for g in range(PASSES)]
+        for dst, src in ((centre[0], cx), (centre[1], cy), (sig, sigma)):
+            nc.sync.dma_start(out=dst[:], in_=src.rearrange(by_feature, p=P, t=PACK))
+        nc.sync.dma_start(out=f_raw[:].rearrange("p h t c -> p h (t c)"), in_=features.rearrange(by_feature, p=P, t=PACK))
+        g_src = grad_out.rearrange("(g p r) o -> g p (r o)", p=P, r=PACK)
+        x_src = x_rows.rearrange("(g p r) k -> g p (r k)", p=P, r=PACK)
+        nc.sync.dma_start(out=g_raw[0][:, : 2 * O], in_=g_src[0, :, : 2 * O])
+        nc.sync.dma_start(out=g_raw[0][:, 2 * O :], in_=g_src[0, :, 2 * O :])
+        nc.sync.dma_start(out=g_raw[1][:], in_=g_src[1])
+        for g in range(PASSES):
+            nc.sync.dma_start(out=x_raw[g][:], in_=x_src[g])
 
+        index = keep.tile([P, W], F32, name="index")
+        nc.gpsimd.iota(index[:], [[1, W]], base=0, channel_multiplier=0, allow_small_or_imprecise_dtypes=True)
+        ident16 = keep.tile([P, P], BF16, name="ident16")
+        make_identity(nc, ident16[:])
+        ident32 = keep.tile([P, P], F32, name="ident32")
+        make_identity(nc, ident32[:])
+        exp_warm = keep.tile([P, W], F32, name="exp_warm")
+        nc.scalar.activation(out=exp_warm[:], in_=index[:], func=ACT.Exp, scale=-1.0)
         grid = keep.tile([P, W], F32, name="grid")
-        nc.gpsimd.iota(grid[:], [[1, W]], base=0, channel_multiplier=0, allow_small_or_imprecise_dtypes=True)
-        id16 = keep.tile([P, P], BF16, name="id16")
-        make_identity(nc, id16[:])
-        id32 = keep.tile([P, P], F32, name="id32")
-        make_identity(nc, id32[:])
-        scratch = keep.tile([P, W], F32, name="scratch")
-        nc.scalar.activation(out=scratch[:], in_=grid[:], func=ACT.Exp, scale=-1.0)
-        gridc = keep.tile([P, W], F32, name="gridc")
-        nc.vector.tensor_scalar(out=gridc[:], in0=grid[:], scalar1=-(W - 1) / 2.0, scalar2=None, op0=ALU.add)
-        if WARM:
-            wsrc = keep.tile([P, 512], BF16, name="wsrc")
-            nc.vector.memset(wsrc[:], 0.0)
-            wb = psum.tile([P, 512], F32, name="warm", tag="bank")
-            for rep in range(WARM0):
-                nc.tensor.matmul(wb[:], lhsT=id16[:], rhs=wsrc[:], start=True, stop=True)
+        nc.vector.tensor_scalar(out=grid[:], in0=index[:], scalar1=-(W - 1) / 2.0, scalar2=None, op0=ALU.add)
 
-        s2 = keep.tile([P, 2, 8], F32, name="s2")
-        sgb = sg[:].unsqueeze(1).to_broadcast([P, 2, 8])
-        nc.vector.tensor_tensor(out=s2[:], in0=sgb, in1=sgb, op=ALU.mult)
-        d = keep.tile([P, 2, 2, W, 4], F32, name="d")
+        warm_bank = psum.tile([P, P], F32, name="warm_bank", tag="bank")
+
+        def warm_up():
+            for rep in range(WARM_UP):
+                nc.tensor.matmul(warm_bank[:], lhsT=ident16[:], rhs=ident16[:], start=True, stop=True)
+
+        warm_up()
+
+        axis_shape = [P, PASSES, W, PACK]
+        sig2 = keep.tile([P, 2, PASSES * PACK], F32, name="sig2")
+        sig_twice = sig[:].rearrange("p h t -> p (h t)").unsqueeze(1).to_broadcast([P, 2, PASSES * PACK])
+        nc.vector.tensor_tensor(out=sig2[:], in0=sig_twice, in1=sig_twice, op=ALU.mult)
+        dist = keep.tile([P, 2, PASSES, W, PACK], F32, name="dist")
         for a in range(2):
-            nc.vector.tensor_tensor(out=d[:, a], in0=cen[a][:].unsqueeze(2).to_broadcast([P, 2, W, 4]),
-                                    in1=gridc[:].unsqueeze(1).unsqueeze(3).to_broadcast([P, 2, W, 4]), op=ALU.subtract)
-        r2 = keep.tile([P, 16], F32, name="r2")
-        nc.vector.reciprocal(out=r2[:], in_=s2[:].rearrange("p a q -> p (a q)"))
-        d2 = keep.tile([P, 4, W, 4], F32, name="d2")
-        dv = d[:].rearrange("p a h i t -> p (a h) i t")
-        nc.vector.tensor_tensor(out=d2[:], in0=dv, in1=dv, op=ALU.mult)
-        arg = keep.tile([P, 4, W, 4], F32, name="arg")
-        nc.vector.tensor_tensor(out=arg[:], in0=d2[:], in1=r2[:].rearrange("p (q t) -> p q t", t=4).unsqueeze(2).to_broadcast([P, 4, W, 4]), op=ALU.mult)
-        e = keep.tile([P, 2, 2, W, 4], F32, name="e")
-        nc.scalar.activation(out=e[:].rearrange("p a h i t -> p (a h i t)"), in_=arg[:].rearrange("p q i t -> p (q i t)"), func=ACT.Exp, scale=-1.0)
+            nc.vector.tensor_tensor(
+                out=dist[:, a],
+                in0=centre[a][:].unsqueeze(2).to_broadcast(axis_shape),
+                in1=grid[:].unsqueeze(1).unsqueeze(3).to_broadcast(axis_shape),
+                op=ALU.subtract,
+            )
+        inv_sig2 = keep.tile([P, 2 * PASSES * PACK], F32, name="inv_sig2")
+        nc.vector.reciprocal(out=inv_sig2[:], in_=sig2[:].rearrange("p a q -> p (a q)"))
+        both_shape = [P, 2 * PASSES, W, PACK]
+        dist_both = dist[:].rearrange("p a h i t -> p (a h) i t")
+        dist2 = keep.tile(both_shape, F32, name="dist2")
+        nc.vector.tensor_tensor(out=dist2[:], in0=dist_both, in1=dist_both, op=ALU.mult)
+        scaled = keep.tile(both_shape, F32, name="scaled")
+        nc.vector.tensor_tensor(
+            out=scaled[:],
+            in0=dist2[:],
+            in1=inv_sig2[:].rearrange("p (q t) -> p q t", t=PACK).unsqueeze(2).to_broadcast(both_shape),
+            op=ALU.mult,
+        )
+        gauss = keep.tile([P, 2, PASSES, W, PACK], F32, name="gauss")
+        nc.scalar.activation(
+            out=gauss[:].rearrange("p a h i t -> p (a h i t)"),
+            in_=scaled[:].rearrange("p q i t -> p (q i t)"),
+            func=ACT.Exp,
+            scale=-1.0,
+        )
 
-        f_ps = fpsum.tile([P, 2, C, 4], F32, name="f_ps")
-        nc.tensor.matmul(f_ps[:].rearrange("p h c t -> p (h c t)"), lhsT=id16[:], rhs=f_raw[:].rearrange("p h t c -> p h c t"), start=True, stop=True)
-        for rep in range(WARM - WARM0):
-            nc.tensor.matmul(wb[:], lhsT=id16[:], rhs=wsrc[:], start=True, stop=True)
-        f_sb = keep.tile([P, 2, C, 4], F32, name="f_sb")
-        nc.scalar.copy(out=f_sb[:], in_=f_ps[:])
-        sp = keep.tile([P, 2, W, H, 4], F32, name="sp")
-        for h in range(2):
-            nc.vector.tensor_tensor(out=sp[:, h], in0=e[:, 0, h].unsqueeze(2).to_broadcast([P, W, H, 4]),
-                                    in1=e[:, 1, h].unsqueeze(1).to_broadcast([P, W, H, 4]), op=ALU.mult)
-        ey = keep.tile([P, 2, 4, H], F32, name="ey")
+        f_psum = fpsum.tile([P, PASSES, C, PACK], F32, name="f_psum")
+        nc.tensor.matmul(
+            f_psum[:].rearrange("p h c t -> p (h c t)"),
+            lhsT=ident16[:],
+            rhs=f_raw[:].rearrange("p h t c -> p h c t"),
+            start=True,
+            stop=True,
+        )
+        warm_up()
+        f_sbuf = keep.tile([P, PASSES, C, PACK], F32, name="f_sbuf")
+        nc.scalar.copy(out=f_sbuf[:], in_=f_psum[:])
+        spatial = keep.tile([P, PASSES, W, H, PACK], F32, name="spatial")
+        for h in range(PASSES):
+            nc.vector.tensor_tensor(
+                out=spatial[:, h],
+                in0=gauss[:, 0, h].unsqueeze(2).to_broadcast([P, W, H, PACK]),
+                in1=gauss[:, 1, h].unsqueeze(1).to_broadcast([P, W, H, PACK]),
+                op=ALU.mult,
+            )
 
-        gt_bf = keep.tile([P, 8, 1024], BF16, name="gt_bf", align_bytes=64)
-        gt_c = keep.tile([P, 8, 2, P], U32, name="gt_c", align_bytes=64)
-        gt_s = keep.tile([P, 8, 2, P], U8, name="gt_s", align_bytes=64)
-        gi_bf = [keep.tile([P, 4 * O], BF16, name="gi_bf%d" % g, align_bytes=64) for g in range(2)]
-        gi_c = keep.tile([P, 2, O], U32, name="gi_c", align_bytes=64)
-        gi_s = keep.tile([P, 2, O], U8, name="gi_s", align_bytes=64)
-        w_c = [keep.tile([P, 2, 512], U32, name="w_c%d" % n, align_bytes=64) for n in range(4)]
-        w_s = [keep.tile([P, 2, 512], U8, name="w_s%d" % n, align_bytes=64) for n in range(4)]
-        x_c = [keep.tile([P, 2, 512], U32, name="x_c%d" % n, align_bytes=64) for n in range(4)]
-        x_s = [keep.tile([P, 2, 512], U8, name="x_s%d" % n, align_bytes=64) for n in range(4)]
-        acc = [keep.tile([P, C * H], F32, name="acc%d" % q) for q in range(8)]
-        df = keep.tile([P, 2, 4, C], F32, name="df")
+        go_bf = keep.tile([P, ROW_TILES, PASSES * P * PACK], BF16, name="go_bf", align_bytes=64)
+        go_codes = keep.tile([P, ROW_TILES, PASSES, P], U32, name="go_codes", align_bytes=64)
+        go_scales = keep.tile([P, ROW_TILES, PASSES, P], U8, name="go_scales", align_bytes=64)
+        gb_bf = [keep.tile([P, O * PACK], BF16, name="gb_bf%d" % g, align_bytes=64) for g in range(PASSES)]
+        gb_codes = keep.tile([P, PASSES, O], U32, name="gb_codes", align_bytes=64)
+        gb_scales = keep.tile([P, PASSES, O], U8, name="gb_scales", align_bytes=64)
+        w_codes = [keep.tile([P, PASSES, N], U32, name="w_codes%d" % n, align_bytes=64) for n in range(COL_TILES)]
+        w_scales = [keep.tile([P, PASSES, N], U8, name="w_scales%d" % n, align_bytes=64) for n in range(COL_TILES)]
+        x_codes = [keep.tile([P, PASSES, N], U32, name="x_codes%d" % n, align_bytes=64) for n in range(COL_TILES)]
+        x_scales = [keep.tile([P, PASSES, N], U8, name="x_scales%d" % n, align_bytes=64) for n in range(COL_TILES)]
+        sum_i = [keep.tile([P, CJ], F32, name="sum_i%d" % q) for q in range(ROW_TILES)]
+        ey = keep.tile([P, PASSES, PACK, H], F32, name="ey")
+        d_features = keep.tile([P, PASSES, PACK, C], F32, name="d_features")
         w_bf = {}
         x_bf = {}
-        banks = {}
+        dw_bank = {}
+        times_ey = {}
 
-        def transposes(m):
-            g, j = divmod(m, 4)
+        def transpose_g(m):
+            g, r = divmod(m, PACK)
             words = g_raw[g][:].bitcast(F32)
-            bank = psum.tile([P, 2, 2, P], F32, name="tr%d" % m, tag="bank")
-            for h in range(2):
+            bank = psum.tile([P, PASSES, 2, P], F32, name="go_bank%d" % m, tag="bank")
+            for h in range(PASSES):
+                first = (O * r + PASS * h) // 2
                 for u in range(2):
-                    lo = 512 * j + 256 * h
-                    nc.tensor.transpose(bank[:, h, u, :], words[:, lo + u:lo + 256:2], id32[:])
-            nc.scalar.copy(out=gt_bf[:, m, :].bitcast(F32).rearrange("p (h r u) -> p h r u", h=2, u=2),
-                           in_=bank[:].rearrange("p h u r -> p h r u"))
+                    nc.tensor.transpose(bank[:, h, u, :], words[:, first + u : first + PASS // 2 : 2], ident32[:])
+            nc.scalar.copy(
+                out=go_bf[:, m, :].bitcast(F32).rearrange("p (h b u) -> p h b u", h=PASSES, u=2),
+                in_=bank[:].rearrange("p h u b -> p h b u"),
+            )
 
-        def quant_gt(m0, cnt):
-            nc.vector.quantize_mx(out=gt_c[:, m0:m0 + cnt].rearrange("p m h r -> p (m h r)").bitcast(E5),
-                                  scales=gt_s[:, m0:m0 + cnt].rearrange("p m h r -> p (m h r)"),
-                                  in_=gt_bf[:, m0:m0 + cnt, :].rearrange("p m w -> p (m w)"))
+        def quantise_go(first, count):
+            tiles = slice(first, first + count)
+            nc.vector.quantize_mx(
+                out=go_codes[:, tiles].rearrange("p m h b -> p (m h b)").bitcast(E5M2),
+                scales=go_scales[:, tiles].rearrange("p m h b -> p (m h b)"),
+                in_=go_bf[:, tiles, :].rearrange("p m w -> p (m w)"),
+            )
 
-        def inter_g_pe(g, h, tp):
-            bank = psum.tile([P, 2, 512], BF16, name="ig%d%d%d" % (g, h, tp), tag="bank")
-            src = g_raw[g][:].rearrange("p (j h m t) -> p h t m j", j=4, h=2, t=4)
-            for tt in range(2):
-                nc.tensor.matmul(bank[:, tt, :], lhsT=id16[:], rhs=src[:, h, 2 * tp + tt], start=True, stop=True)
-            lo = 2048 * h + 1024 * tp
-            nc.scalar.copy(out=gi_bf[g][:, lo:lo + 1024], in_=bank[:].rearrange("p a b -> p (a b)"))
+        def interleave_g(g, quarter):
+            h, half = divmod(quarter, 2)
+            bank = psum.tile([P, PACK, 64, PACK], BF16, name="gb_bank%d%d" % (g, quarter), tag="bank")
+            src = g_raw[g][:].rearrange("p (r o) -> p o r", r=PACK)
+            for part in range(2):
+                first = 256 * quarter + P * part
+                nc.tensor.matmul(
+                    bank[:, :, 32 * part : 32 * (part + 1), :].rearrange("p t m r -> p m t r"),
+                    lhsT=ident16[:],
+                    rhs=src[:, first : first + P, :],
+                    start=True,
+                    stop=True,
+                )
+            dst = gb_bf[g][:].rearrange("p (h t half w) -> p h half t w", h=PASSES, t=PACK, half=2)
+            nc.scalar.copy(out=dst[:, h, half], in_=bank[:].rearrange("p t m r -> p t (m r)"))
 
-        def inter_g(g, h, eng):
-            src = g_raw[g][:].rearrange("p (j h mp m t) -> p h mp t m j", j=4, h=2, m=2, t=4)[:, h]
-            dst = gi_bf[g][:].rearrange("p (h t mp m j) -> p h mp t m j", j=4, h=2, m=2, t=4)[:, h]
-            if eng == 'S':
-                nc.scalar.copy(out=dst, in_=src)
-            else:
-                nc.vector.tensor_copy(out=dst, in_=src)
+        def quantise_gb(g):
+            nc.vector.quantize_mx(out=gb_codes[:, g, :].bitcast(E5M2), scales=gb_scales[:, g, :], in_=gb_bf[g][:])
 
-        def quant_gi(g):
-            nc.vector.quantize_mx(out=gi_c[:, g, :].bitcast(E5), scales=gi_s[:, g, :], in_=gi_bf[g][:])
+        def build_w(n, h, channels, engine, f_src):
+            shape = [P, len(channels), S, PACK]
+            engine.tensor_tensor(
+                out=w_bf[n, h][:, channels.start : channels.stop],
+                in0=f_src[:, h, TILE_C * n + channels.start : TILE_C * n + channels.stop, :]
+                .unsqueeze(2)
+                .to_broadcast(shape),
+                in1=spatial[:, h].rearrange("p i j t -> p (i j) t").unsqueeze(1).to_broadcast(shape),
+                op=ALU.mult,
+            )
 
-        def build_w(n, h, c0, c1, eng):
-            if (n, h) not in w_bf:
-                w_bf[n, h] = stage.tile([P, 8, S, 4], BF16, name="w_bf%d%d" % (n, h), tag="w_bf" + eng, bufs=WB[eng], align_bytes=64)
-            if c1 <= c0:
-                return
-            shape = [P, c1 - c0, S, 4]
-            spb = sp[:, h].rearrange("p i j t -> p (i j) t").unsqueeze(1).to_broadcast(shape)
-            src = f_ps if eng == 'V' else f_sb
-            fb = src[:, h, 8 * n + c0:8 * n + c1, :].unsqueeze(2).to_broadcast(shape)
-            (nc.vector if eng == 'V' else nc.gpsimd).tensor_tensor(out=w_bf[n, h][:, c0:c1], in0=fb, in1=spb, op=ALU.mult)
+        def build_w_gpsimd(n, h):
+            w_bf[n, h] = stage.tile([P, TILE_C, S, PACK], BF16, name="w_bf%d%d" % (n, h), tag="w_gpsimd", align_bytes=64)
+            build_w(n, h, range(GPSIMD_CHANNELS[n, h]), nc.gpsimd, f_sbuf)
 
-        def quant_w(n, h):
-            nc.vector.quantize_mx(out=w_c[n][:, h, :].bitcast(E4), scales=w_s[n][:, h, :], in_=w_bf[n, h][:].rearrange("p c s t -> p (c s t)"))
+        def build_w_vector(n, h):
+            if (n, h) not in GPSIMD_CHANNELS:
+                w_bf[n, h] = stage.tile([P, TILE_C, S, PACK], BF16, name="w_bf%d%d" % (n, h), align_bytes=64)
+            build_w(n, h, range(GPSIMD_CHANNELS.get((n, h), 0), TILE_C), nc.vector, f_psum)
 
-        def inter_x(n, g, i0, i1, eng):
-            if (n, g) not in x_bf:
-                x_bf[n, g] = stage.tile([P, 2, C, H, 4], BF16, name="x_bf%d%d" % (n, g), tag="x_bf", bufs=4, align_bytes=64)
-            src = x_raw[g][:].rearrange("p (t c i j) -> p i c j t", t=4, i=W, j=H)[:, 2 * n + i0:2 * n + i1]
-            dst = x_bf[n, g][:, i0:i1]
-            if eng == 'S':
-                nc.scalar.copy(out=dst, in_=src)
-            elif eng == 'V':
-                nc.vector.tensor_copy(out=dst, in_=src)
-            else:
-                nc.gpsimd.tensor_scalar(out=dst, in0=src, scalar1=1.0, scalar2=0.0, op0=ALU.mult, op1=ALU.add)
+        def quantise_w(n, h):
+            nc.vector.quantize_mx(
+                out=w_codes[n][:, h, :].bitcast(E4M3),
+                scales=w_scales[n][:, h, :],
+                in_=w_bf[n, h][:].rearrange("p c s t -> p (c s t)"),
+            )
 
-        def quant_x(n, g):
-            nc.vector.quantize_mx(out=x_c[n][:, g, :].bitcast(E4), scales=x_s[n][:, g, :], in_=x_bf[n, g][:].rearrange("p i c j t -> p (i c j t)"))
+        def x_piece(n, g, i):
+            if n not in x_bf:
+                x_bf[n] = stage.tile(
+                    [P, PASSES, TILE_I, C, H, PACK], BF16, name="x_bf%d" % n, tag="x_bf", bufs=3, align_bytes=64
+                )
+            src = x_raw[g][:].rearrange("p (r c i j) -> p i c j r", r=PACK, i=W, j=H)[:, TILE_I * n + i]
+            return src, x_bf[n][:, g, i]
 
-        def dx(n, m):
-            bank = psum.tile([P, 512], F32, name="dx%d%d" % (n, m), tag="bank")
-            for h in range(2):
-                nc.tensor.matmul_mx(out=bank[:], lhsT=gt_c[:, m, h, :].bitcast(E5), lhsT_scale=gt_s[:, m, h, :],
-                                    rhs=w_c[n][:, h, :].bitcast(E4), rhs_scale=w_s[n][:, h, :], start=h == 0, stop=h == 1)
-            res = outp.tile([P, 512], F32, name="res%d%d" % (n, m), tag="res")
-            nc.scalar.copy(out=res[:], in_=bank[:])
-            nc.sync.dma_start(out=dxf[m // 4, m % 4, :, 512 * n:512 * (n + 1)], in_=res[:])
+        def interleave_x_tensor(n, g, i):
+            src, dst = x_piece(n, g, i)
+            bank = psum.tile([P, 2, N], BF16, name="x_bank%d%d%d" % (n, g, i), tag="bank")
+            for part in range(2):
+                channels = slice(C // 2 * part, C // 2 * (part + 1))
+                nc.tensor.matmul(bank[:, part, :], lhsT=ident16[:], rhs=src[:, channels], start=True, stop=True)
+            nc.scalar.copy(out=dst.rearrange("p c j r -> p (c j r)"), in_=bank[:].rearrange("p a w -> p (a w)"))
 
-        def dw_mm(n, q):
-            bank = psum.tile([P, 512], F32, name="dw%d%d" % (n, q), tag="bank")
-            banks[n, q] = bank
+        def interleave_x_vector(n, g, i):
+            src, dst = x_piece(n, g, i)
+            nc.vector.tensor_copy(out=dst, in_=src)
+
+        def interleave_x_scalar(n, g, i):
+            src, dst = x_piece(n, g, i)
+            nc.scalar.copy(out=dst, in_=src)
+
+        def quantise_x(n):
+            nc.vector.quantize_mx(
+                out=x_codes[n][:].rearrange("p g w -> p (g w)").bitcast(E4M3),
+                scales=x_scales[n][:].rearrange("p g w -> p (g w)"),
+                in_=x_bf[n][:].rearrange("p g i c j r -> p (g i c j r)"),
+            )
+
+        def out_0_tile(n, m):
+            bank = psum.tile([P, N], F32, name="dx_bank%d%d" % (n, m), tag="bank")
+            for h in range(PASSES):
+                nc.tensor.matmul_mx(
+                    out=bank[:],
+                    lhsT=go_codes[:, m, h, :].bitcast(E5M2),
+                    lhsT_scale=go_scales[:, m, h, :],
+                    rhs=w_codes[n][:, h, :].bitcast(E4M3),
+                    rhs_scale=w_scales[n][:, h, :],
+                    start=h == 0,
+                    stop=h == PASSES - 1,
+                )
+            result = stage.tile([P, N], F32, name="result%d%d" % (n, m), tag="result", bufs=RESULT_BUFS)
+            nc.scalar.copy(out=result[:], in_=bank[:])
+            nc.sync.dma_start(out=out_0_tiles[m // PACK, m % PACK, :, N * n : N * (n + 1)], in_=result[:])
+
+        def dweight_tile(n, q):
+            dw_bank[n, q] = psum.tile([P, TILE_I, CJ], F32, name="dw_bank%d%d" % (n, q), tag="bank")
             cols = slice(P * q, P * (q + 1))
-            for g in range(2):
-                nc.tensor.matmul_mx(out=bank[:], lhsT=gi_c[:, g, cols].bitcast(E5), lhsT_scale=gi_s[:, g, cols],
-                                    rhs=x_c[n][:, g, :].bitcast(E4), rhs_scale=x_s[n][:, g, :], start=g == 0, stop=g == 1)
+            for g in range(PASSES):
+                nc.tensor.matmul_mx(
+                    out=dw_bank[n, q][:].rearrange("p i w -> p (i w)"),
+                    lhsT=gb_codes[:, g, cols].bitcast(E5M2),
+                    lhsT_scale=gb_scales[:, g, cols],
+                    rhs=x_codes[n][:, g, :].bitcast(E4M3),
+                    rhs_scale=x_scales[n][:, g, :],
+                    start=g == 0,
+                    stop=g == PASSES - 1,
+                )
 
-        def fold(n, q, i2):
-            i = 2 * n + i2
-            part = banks[n, q][:, 256 * i2:256 * (i2 + 1)]
-            ex = e[:, 0, q // 4, i, q % 4:q % 4 + 1]
-            if i == 0:
-                if E1S:
-                    nc.scalar.activation(out=acc[q][:], in_=part, func=ACT.Copy, scale=ex)
-                else:
-                    nc.vector.tensor_scalar(out=acc[q][:], in0=part, scalar1=ex, scalar2=None, op0=ALU.mult)
+        def add_row(n, q, i):
+            h, t = divmod(q, PACK)
+            row = TILE_I * n + i
+            ex = gauss[:, 0, h, row, t : t + 1]
+            if row == 0:
+                nc.vector.tensor_scalar(out=sum_i[q][:], in0=dw_bank[n, q][:, i], scalar1=ex, scalar2=None, op0=ALU.mult)
             else:
-                nc.vector.scalar_tensor_tensor(out=acc[q][:], in0=part, scalar=ex, in1=acc[q][:], op0=ALU.mult, op1=ALU.add)
+                nc.vector.scalar_tensor_tensor(
+                    out=sum_i[q][:], in0=dw_bank[n, q][:, i], scalar=ex, in1=sum_i[q][:], op0=ALU.mult, op1=ALU.add
+                )
 
-        prods = {}
+        def multiply_ey(q):
+            engine = nc.vector if q == ROW_TILES - 1 else nc.gpsimd
+            times_ey[q] = stage.tile([P, C, H], F32, name="times_ey%d" % q, tag="times_ey", bufs=REDUCE_LAG + 2)
+            engine.tensor_tensor(
+                out=times_ey[q][:],
+                in0=sum_i[q][:].rearrange("p (c j) -> p c j", j=H),
+                in1=ey[:, q // PACK, q % PACK, :].unsqueeze(1).to_broadcast([P, C, H]),
+                op=ALU.mult,
+            )
 
-        def fin_mul(q):
-            prods[q] = stage.tile([P, C, H], F32, name="prod%d" % q, tag="prod", bufs=4)
-            (nc.gpsimd if E2G and q < 7 else nc.vector).tensor_tensor(
-                out=prods[q][:], in0=acc[q][:].rearrange("p (c j) -> p c j", j=H),
-                in1=ey[:, q // 4, q % 4, :].unsqueeze(1).to_broadcast([P, C, H]), op=ALU.mult)
+        def reduce_j(q):
+            nc.vector.tensor_reduce(
+                out=d_features[:, q // PACK, q % PACK, :], in_=times_ey[q][:], axis=mybir.AxisListType.X, op=ALU.add
+            )
 
-        def fin_red(q):
-            nc.vector.tensor_reduce(out=df[:, q // 4, q % 4, :], in_=prods[q][:], axis=mybir.AxisListType.X, op=ALU.add)
+        build_w_gpsimd(1, 1)
+        build_w_vector(0, 0)
+        build_w_vector(1, 1)
+        build_w_vector(0, 1)
+        for quarter in range(4):
+            transpose_g(2 * quarter)
+            transpose_g(2 * quarter + 1)
+            interleave_g(0, quarter)
+        quantise_w(0, 0)
+        quantise_w(0, 1)
+        quantise_go(0, 2)
+        quantise_go(2, 2)
+        quantise_w(1, 1)
 
-        def ig(g, h):
-            for tp in range(2):
-                inter_g_pe(g, h, tp)
+        out_0_todo = [(n, m) for n in range(COL_TILES) for m in range(ROW_TILES)]
+        build_w_gpsimd(2, 0)
+        build_w_vector(1, 0)
+        build_w_vector(2, 0)
+        for quarter in range(4):
+            interleave_g(1, quarter)
+        for i in range(TILE_I):
+            interleave_x_tensor(0, 0, i)
+        for m in range(PACK):
+            out_0_tile(*out_0_todo.pop(0))
+        quantise_go(PACK, PACK)
+        quantise_w(1, 0)
+        for i in range(TILE_I):
+            interleave_x_vector(0, 1, i)
+        quantise_gb(0)
+        quantise_gb(1)
+        quantise_x(0)
+        quantise_w(2, 0)
+        for m in range(PACK):
+            out_0_tile(*out_0_todo.pop(0))
+        for i in range(TILE_I):
+            interleave_x_tensor(1, 0, i)
+        for m in range(PACK):
+            out_0_tile(*out_0_todo.pop(0))
+        nc.scalar.copy(out=ey[:], in_=gauss[:, 1].rearrange("p h j t -> p h t j"))
 
-        def xi(n, r, engs):
-            if IXE[n][r] in engs:
-                inter_x(n, r // 2, r % 2, r % 2 + 1, IXE[n][r])
-
-        def w(n, h):
-            build_w(n, h, 0, 8, WE[2 * n + h])
-
-        w(1, 1)
-        w(0, 0)
-        w(0, 1)
-        for m in range(4):
-            transposes(m)
-        ig(0, 0)
-        transposes(4)
-        transposes(5)
-        ig(0, 1)
-        transposes(6)
-        transposes(7)
-        quant_w(0, 0)
-        quant_w(0, 1)
-        quant_gt(0, 2)
-        quant_gt(2, 2)
-        quant_w(1, 1)
-        quant_gt(4, 2)
-        quant_gi(0)
-        quant_gt(6, 2)
-        w(1, 0)
-        w(2, 0)
-        w(2, 1)
-        for m in range(4):
-            dx(0, m)
-        ig(1, 0)
-        ig(1, 1)
-        for m in range(4, 8):
-            dx(0, m)
-        quant_w(1, 0)
-        quant_gi(1)
-        for r in range(4):
-            xi(0, r, 'SVG')
-        quant_x(0, 0)
-        quant_x(0, 1)
-        quant_w(2, 0)
-        quant_w(2, 1)
-        todo = [(n, m) for n in range(1, 4) for m in range(8)]
-        for c in range(24 - sum(XB)):
-            dx(*todo.pop(0))
-            if c in PRE:
-                xi(1, PRE.index(c), 'SVG')
-        nc.scalar.copy(out=ey[:], in_=e[:, 1].rearrange("p h j t -> p h t j"))
-        for n in range(4):
-            if n < 2:
-                w(3, n)
-            done = 0
-            for q in range(8):
-                dw_mm(n, q)
-                fold(n, q, 0)
+        x_todo = [(n, g, i) for n in range(1, COL_TILES) for g in range(PASSES) for i in range(TILE_I)][TILE_I:]
+        w_todo = [(2, 1), (3, 0), (3, 1)]
+        last = COL_TILES - 1
+        for n in range(COL_TILES):
+            if n < last:
+                build_w_gpsimd(*w_todo[n])
+            for q in range(ROW_TILES):
+                dweight_tile(n, q)
+                add_row(n, q, 0)
                 if q > 0:
-                    fold(n, q - 1, 1)
-                    if n == 3:
-                        fin_mul(q - 1)
-                if n == 3 and q >= RL:
-                    fin_red(q - RL)
-                if n < 3 and q < 4 and q >= len(PRE):
-                    xi(n + 1, q, 'SVG')
-                if n < 2 and q >= 8 - len(PRE):
-                    xi(n + 2, q - 8 + len(PRE), 'SVG')
-                if n < 3 and q == QX:
-                    quant_x(n + 1, 0)
-                    quant_x(n + 1, 1)
-                    if n < 2:
-                        quant_w(3, n)
-                lim = (XB[n] if n < 3 else L3) * (q + 1) // 8
-                while done < lim:
-                    dx(*todo.pop(0))
-                    done = done + 1
-            fold(n, 7, 1)
-        fin_mul(7)
-        for q in range(8 - RL, 8):
-            fin_red(q)
-        while todo:
-            dx(*todo.pop(0))
-        nc.sync.dma_start(out=out_1.rearrange("(h p t) c a b -> p h (t c a b)", p=P, t=4), in_=df[:].rearrange("p h t c -> p h (t c)"))
+                    add_row(n, q - 1, 1)
+                elif n > 0:
+                    add_row(n - 1, ROW_TILES - 1, 1)
+                if n == last and q > 0:
+                    multiply_ey(q - 1)
+                if n == last and q > REDUCE_LAG:
+                    reduce_j(q - 1 - REDUCE_LAG)
+                if q % 2 == 0 and x_todo:
+                    interleave_x_scalar(*x_todo.pop(0))
+                if n < last and q == QUANTISE_AT:
+                    quantise_x(n + 1)
+                    quantise_w(*w_todo[n])
+                if q % 2 == 1:
+                    out_0_tile(*out_0_todo.pop(0))
+
+        add_row(last, ROW_TILES - 1, 1)
+        multiply_ey(ROW_TILES - 1)
+        for q in range(ROW_TILES - 1 - REDUCE_LAG, ROW_TILES):
+            reduce_j(q)
+        for n, m in out_0_todo:
+            out_0_tile(n, m)
+        nc.sync.dma_start(
+            out=out_1.rearrange(by_feature, p=P, t=PACK), in_=d_features[:].rearrange("p h t c -> p h (t c)")
+        )

@@ -32,7 +32,6 @@ CJ = C * H
 GPSIMD_CHANNELS = {(1, 1): 7, (2, 0): 5, (2, 1): TILE_C, (3, 0): TILE_C, (3, 1): TILE_C}
 QUANTISE_AT = 5
 REDUCE_LAG = 2
-WARM_UP = 8
 RESULT_BUFS = 8
 WORK_BANKS = 7
 
@@ -74,18 +73,8 @@ def tile_gaussianspatialxfeaturelinear_v_kernel(
         make_identity(nc, ident16[:])
         ident32 = keep.tile([P, P], F32, name="ident32")
         make_identity(nc, ident32[:])
-        exp_warm = keep.tile([P, W], F32, name="exp_warm")
-        nc.scalar.activation(out=exp_warm[:], in_=index[:], func=ACT.Exp, scale=-1.0)
         grid = keep.tile([P, W], F32, name="grid")
         nc.vector.tensor_scalar(out=grid[:], in0=index[:], scalar1=-(W - 1) / 2.0, scalar2=None, op0=ALU.add)
-
-        warm_bank = psum.tile([P, P], F32, name="warm_bank", tag="bank")
-
-        def warm_up():
-            for rep in range(WARM_UP):
-                nc.tensor.matmul(warm_bank[:], lhsT=ident16[:], rhs=ident16[:], start=True, stop=True)
-
-        warm_up()
 
         axis_shape = [P, PASSES, W, PACK]
         sig2 = keep.tile([P, 2, PASSES * PACK], F32, name="sig2")
@@ -128,7 +117,6 @@ def tile_gaussianspatialxfeaturelinear_v_kernel(
             start=True,
             stop=True,
         )
-        warm_up()
         f_sbuf = keep.tile([P, PASSES, C, PACK], F32, name="f_sbuf")
         nc.scalar.copy(out=f_sbuf[:], in_=f_psum[:])
         spatial = keep.tile([P, PASSES, W, H, PACK], F32, name="spatial")
@@ -179,21 +167,12 @@ def tile_gaussianspatialxfeaturelinear_v_kernel(
                 in_=go_bf[:, tiles, :].rearrange("p m w -> p (m w)"),
             )
 
-        def interleave_g(g, quarter):
+        def interleave_g(g, quarter, copy):
             h, half = divmod(quarter, 2)
-            bank = psum.tile([P, PACK, 64, PACK], BF16, name="gb_bank%d%d" % (g, quarter), tag="bank")
-            src = g_raw[g][:].rearrange("p (r o) -> p o r", r=PACK)
-            for part in range(2):
-                first = 256 * quarter + P * part
-                nc.tensor.matmul(
-                    bank[:, :, 32 * part : 32 * (part + 1), :].rearrange("p t m r -> p m t r"),
-                    lhsT=ident16[:],
-                    rhs=src[:, first : first + P, :],
-                    start=True,
-                    stop=True,
-                )
-            dst = gb_bf[g][:].rearrange("p (h t half w) -> p h half t w", h=PASSES, t=PACK, half=2)
-            nc.scalar.copy(out=dst[:, h, half], in_=bank[:].rearrange("p t m r -> p t (m r)"))
+            sizes = dict(r=PACK, h=PASSES, half=2, m=2, t=PACK)
+            src = g_raw[g][:].rearrange("p (r h half pair m t) -> p h half pair t m r", **sizes)
+            dst = gb_bf[g][:].rearrange("p (h t half pair m r) -> p h half pair t m r", **sizes)
+            copy(out=dst[:, h, half], in_=src[:, h, half])
 
         def quantise_gb(g):
             nc.vector.quantize_mx(out=gb_codes[:, g, :].bitcast(E5M2), scales=gb_scales[:, g, :], in_=gb_bf[g][:])
@@ -225,29 +204,14 @@ def tile_gaussianspatialxfeaturelinear_v_kernel(
                 in_=w_bf[n, h][:].rearrange("p c s t -> p (c s t)"),
             )
 
-        def x_piece(n, g, i):
+        def interleave_x(n, g, i, copy):
             if n not in x_bf:
                 x_bf[n] = stage.tile(
                     [P, PASSES, TILE_I, C, H, PACK], BF16, name="x_bf%d" % n, tag="x_bf", bufs=3, align_bytes=64
                 )
-            src = x_raw[g][:].rearrange("p (r c i j) -> p i c j r", r=PACK, i=W, j=H)[:, TILE_I * n + i]
-            return src, x_bf[n][:, g, i]
-
-        def interleave_x_tensor(n, g, i):
-            src, dst = x_piece(n, g, i)
-            bank = psum.tile([P, 2, N], BF16, name="x_bank%d%d%d" % (n, g, i), tag="bank")
-            for part in range(2):
-                channels = slice(C // 2 * part, C // 2 * (part + 1))
-                nc.tensor.matmul(bank[:, part, :], lhsT=ident16[:], rhs=src[:, channels], start=True, stop=True)
-            nc.scalar.copy(out=dst.rearrange("p c j r -> p (c j r)"), in_=bank[:].rearrange("p a w -> p (a w)"))
-
-        def interleave_x_vector(n, g, i):
-            src, dst = x_piece(n, g, i)
-            nc.vector.tensor_copy(out=dst, in_=src)
-
-        def interleave_x_scalar(n, g, i):
-            src, dst = x_piece(n, g, i)
-            nc.scalar.copy(out=dst, in_=src)
+            src = x_raw[g][:].rearrange("p (r c i half j) -> p i c half r j", r=PACK, i=W, half=2, j=H // 2)
+            dst = x_bf[n][:, g, i].rearrange("p c (half j) r -> p c half r j", half=2)
+            copy(out=dst, in_=src[:, TILE_I * n + i])
 
         def quantise_x(n):
             nc.vector.quantize_mx(
@@ -316,10 +280,14 @@ def tile_gaussianspatialxfeaturelinear_v_kernel(
         build_w_vector(0, 0)
         build_w_vector(1, 1)
         build_w_vector(0, 1)
-        for quarter in range(4):
+        for m in range(PACK):
+            transpose_g(m)
+        for quarter in range(2):
+            interleave_g(0, quarter, nc.scalar.copy)
+        for quarter in range(2, 4):
             transpose_g(2 * quarter)
             transpose_g(2 * quarter + 1)
-            interleave_g(0, quarter)
+            interleave_g(0, quarter, nc.scalar.copy)
         quantise_w(0, 0)
         quantise_w(0, 1)
         quantise_go(0, 2)
@@ -330,26 +298,26 @@ def tile_gaussianspatialxfeaturelinear_v_kernel(
         build_w_gpsimd(2, 0)
         build_w_vector(1, 0)
         build_w_vector(2, 0)
-        for quarter in range(4):
-            interleave_g(1, quarter)
-        for i in range(TILE_I):
-            interleave_x_tensor(0, 0, i)
-        for m in range(PACK):
+        for m in range(PACK - 1):
             out_0_tile(*out_0_todo.pop(0))
+        for i in range(TILE_I):
+            interleave_x(0, 0, i, nc.scalar.copy)
+        out_0_tile(*out_0_todo.pop(0))
         quantise_go(PACK, PACK)
         quantise_w(1, 0)
+        for quarter in range(4):
+            interleave_g(1, quarter, nc.vector.tensor_copy)
         for i in range(TILE_I):
-            interleave_x_vector(0, 1, i)
+            interleave_x(0, 1, i, nc.vector.tensor_copy)
         quantise_gb(0)
         quantise_gb(1)
         quantise_x(0)
         quantise_w(2, 0)
-        for m in range(PACK):
+        for m in range(ROW_TILES - 1):
             out_0_tile(*out_0_todo.pop(0))
-        for i in range(TILE_I):
-            interleave_x_tensor(1, 0, i)
-        for m in range(PACK):
-            out_0_tile(*out_0_todo.pop(0))
+        interleave_x(1, 0, 0, nc.scalar.copy)
+        out_0_tile(*out_0_todo.pop(0))
+        interleave_x(1, 0, 1, nc.scalar.copy)
         nc.scalar.copy(out=ey[:], in_=gauss[:, 1].rearrange("p h j t -> p h t j"))
 
         x_todo = [(n, g, i) for n in range(1, COL_TILES) for g in range(PASSES) for i in range(TILE_I)][TILE_I:]
@@ -370,7 +338,7 @@ def tile_gaussianspatialxfeaturelinear_v_kernel(
                 if n == last and q > REDUCE_LAG:
                     reduce_j(q - 1 - REDUCE_LAG)
                 if q % 2 == 0 and x_todo:
-                    interleave_x_scalar(*x_todo.pop(0))
+                    interleave_x(*x_todo.pop(0), nc.scalar.copy)
                 if n < last and q == QUANTISE_AT:
                     quantise_x(n + 1)
                     quantise_w(*w_todo[n])

@@ -29,9 +29,10 @@ TILE_C = C // COL_TILES
 TILE_I = W // COL_TILES
 CJ = C * H
 
-GPSIMD_CHANNELS = {(1, 1): 7, (2, 0): 5, (2, 1): TILE_C, (3, 0): TILE_C, (3, 1): TILE_C}
+GPSIMD_CHANNELS = {(1, 1): 7, (2, 0): 4, (2, 1): 7, (3, 0): 7, (3, 1): 7}
 QUANTISE_AT = 5
 REDUCE_LAG = 2
+OUT_0_HELD_BACK = 2
 RESULT_BUFS = 8
 WORK_BANKS = 7
 
@@ -56,9 +57,11 @@ def tile_gaussianspatialxfeaturelinear_v_kernel(
         f_raw = keep.tile([P, PASSES, PACK, C], BF16, name="f_raw")
         g_raw = [keep.tile([P, PACK * O], BF16, name="g_raw%d" % g, align_bytes=64) for g in range(PASSES)]
         x_raw = [keep.tile([P, PACK * K], BF16, name="x_raw%d" % g, align_bytes=64) for g in range(PASSES)]
-        for dst, src in ((centre[0], cx), (centre[1], cy), (sig, sigma)):
-            nc.sync.dma_start(out=dst[:], in_=src.rearrange(by_feature, p=P, t=PACK))
-        nc.sync.dma_start(out=f_raw[:].rearrange("p h t c -> p h (t c)"), in_=features.rearrange(by_feature, p=P, t=PACK))
+        for queue, dst, src in ((nc.sync, sig, sigma), (nc.scalar, centre[0], cx), (nc.sync, centre[1], cy)):
+            queue.dma_start(out=dst[:], in_=src.rearrange(by_feature, p=P, t=PACK))
+        nc.scalar.dma_start(
+            out=f_raw[:].rearrange("p h t c -> p h (t c)"), in_=features.rearrange(by_feature, p=P, t=PACK)
+        )
         g_src = grad_out.rearrange("(g p r) o -> g p (r o)", p=P, r=PACK)
         x_src = x_rows.rearrange("(g p r) k -> g p (r k)", p=P, r=PACK)
         nc.sync.dma_start(out=g_raw[0][:, : 2 * O], in_=g_src[0, :, : 2 * O])
@@ -280,11 +283,7 @@ def tile_gaussianspatialxfeaturelinear_v_kernel(
         build_w_vector(0, 0)
         build_w_vector(1, 1)
         build_w_vector(0, 1)
-        for m in range(PACK):
-            transpose_g(m)
-        for quarter in range(2):
-            interleave_g(0, quarter, nc.scalar.copy)
-        for quarter in range(2, 4):
+        for quarter in range(4):
             transpose_g(2 * quarter)
             transpose_g(2 * quarter + 1)
             interleave_g(0, quarter, nc.scalar.copy)
@@ -313,7 +312,7 @@ def tile_gaussianspatialxfeaturelinear_v_kernel(
         quantise_gb(1)
         quantise_x(0)
         quantise_w(2, 0)
-        for m in range(ROW_TILES - 1):
+        for m in range(PACK + ROW_TILES - OUT_0_HELD_BACK - 1):
             out_0_tile(*out_0_todo.pop(0))
         interleave_x(1, 0, 0, nc.scalar.copy)
         out_0_tile(*out_0_todo.pop(0))
@@ -326,6 +325,8 @@ def tile_gaussianspatialxfeaturelinear_v_kernel(
         for n in range(COL_TILES):
             if n < last:
                 build_w_gpsimd(*w_todo[n])
+                build_w_vector(*w_todo[n])
+            out_0_every = ROW_TILES // OUT_0_HELD_BACK if n == 0 else 2
             for q in range(ROW_TILES):
                 dweight_tile(n, q)
                 add_row(n, q, 0)
@@ -342,7 +343,7 @@ def tile_gaussianspatialxfeaturelinear_v_kernel(
                 if n < last and q == QUANTISE_AT:
                     quantise_x(n + 1)
                     quantise_w(*w_todo[n])
-                if q % 2 == 1:
+                if (q + 1) % out_0_every == 0:
                     out_0_tile(*out_0_todo.pop(0))
 
         add_row(last, ROW_TILES - 1, 1)

from contextlib import ExitStack

import concourse.mybir as mybir
from concourse.masks import make_identity

B, C, W, H, O = 1024, 32, 8, 8, 1024
S = W * H
K = C * S
FLOPS = 2 * 2 * B * O * K
BYTES = 2 * (B * K + B * O + O * C + 3 * O) + 4 * (B * K + O * C)

F32 = mybir.dt.float32
BF16 = mybir.dt.bfloat16
U32 = mybir.dt.uint32
U8 = mybir.dt.uint8
E4M3 = mybir.dt.float8_e4m3fn_x4
E5M2 = mybir.dt.float8_e5m2_x4
ALU = mybir.AluOpType
ACT = mybir.ActivationFunctionType

P = 128
PACK = 4
PASS = P * PACK
PASSES = 2
N = 512
COL_TILES = K // N
ROW_TILES = 8
TILE_C = C // COL_TILES
TILE_I = W // COL_TILES
CJ = C * H

GPSIMD_CHANNELS = {(1, 1): 7, (2, 0): 4, (2, 1): 7, (3, 0): 7, (3, 1): 7}
QUANTISE_AT = 5
REDUCE_LAG = 2
OUT_0_HELD_BACK = 2
RESULT_BUFS = 8
WORK_BANKS = 7


def tile_gaussianspatialxfeaturelinear_v_kernel(
    tc, x, cx, cy, sigma, features, bias, grad_out, out_0, out_1
):
    nc = tc.nc
    x_rows = x.rearrange("b c i j -> b (c i j)")
    out_0_tiles = out_0.rearrange("(g p r) c i j -> g r p (c i j)", p=P, r=PACK)
    by_feature = "(h p t) a b c -> p h (t a b c)"

    with ExitStack() as ctx:
        keep = ctx.enter_context(tc.tile_pool(name="keep", bufs=1))
        stage = ctx.enter_context(tc.tile_pool(name="stage", bufs=1))
        fpsum = ctx.enter_context(tc.psum_pool(name="fpsum", bufs=1))
        psum = ctx.enter_context(tc.psum_pool(name="psum", bufs=WORK_BANKS))
        ctx.enter_context(tc.manual_schedule())

        centre = [keep.tile([P, PASSES, PACK], BF16, name="centre%d" % a) for a in range(2)]
        sig = keep.tile([P, PASSES, PACK], BF16, name="sig")
        f_raw = keep.tile([P, PASSES, PACK, C], BF16, name="f_raw")
        g_raw = [keep.tile([P, PACK * O], BF16, name="g_raw%d" % g, align_bytes=64) for g in range(PASSES)]
        x_raw = [keep.tile([P, PACK * K], BF16, name="x_raw%d" % g, align_bytes=64) for g in range(PASSES)]
        for queue, dst, src in ((nc.sync, sig, sigma), (nc.scalar, centre[0], cx), (nc.sync, centre[1], cy)):
            queue.dma_start(out=dst[:], in_=src.rearrange(by_feature, p=P, t=PACK))
        nc.scalar.dma_start(
            out=f_raw[:].rearrange("p h t c -> p h (t c)"), in_=features.rearrange(by_feature, p=P, t=PACK)
        )
        g_src = grad_out.rearrange("(g p r) o -> g p (r o)", p=P, r=PACK)
        x_src = x_rows.rearrange("(g p r) k -> g p (r k)", p=P, r=PACK)
        nc.sync.dma_start(out=g_raw[0][:, : 2 * O], in_=g_src[0, :, : 2 * O])
        nc.sync.dma_start(out=g_raw[0][:, 2 * O :], in_=g_src[0, :, 2 * O :])
        nc.sync.dma_start(out=g_raw[1][:], in_=g_src[1])
        for g in range(PASSES):
            nc.sync.dma_start(out=x_raw[g][:], in_=x_src[g])

        index = keep.tile([P, W], F32, name="index")
        nc.gpsimd.iota(index[:], [[1, W]], base=0, channel_multiplier=0, allow_small_or_imprecise_dtypes=True)
        ident16 = keep.tile([P, P], BF16, name="ident16")
        make_identity(nc, ident16[:])
        ident32 = keep.tile([P, P], F32, name="ident32")
        make_identity(nc, ident32[:])
        grid = keep.tile([P, W], F32, name="grid")
        nc.vector.tensor_scalar(out=grid[:], in0=index[:], scalar1=-(W - 1) / 2.0, scalar2=None, op0=ALU.add)

        axis_shape = [P, PASSES, W, PACK]
        sig2 = keep.tile([P, 2, PASSES * PACK], F32, name="sig2")
        sig_twice = sig[:].rearrange("p h t -> p (h t)").unsqueeze(1).to_broadcast([P, 2, PASSES * PACK])
        nc.vector.tensor_tensor(out=sig2[:], in0=sig_twice, in1=sig_twice, op=ALU.mult)
        dist = keep.tile([P, 2, PASSES, W, PACK], F32, name="dist")
        for a in range(2):
            nc.vector.tensor_tensor(
                out=dist[:, a],
                in0=centre[a][:].unsqueeze(2).to_broadcast(axis_shape),
                in1=grid[:].unsqueeze(1).unsqueeze(3).to_broadcast(axis_shape),
                op=ALU.subtract,
            )
        inv_sig2 = keep.tile([P, 2 * PASSES * PACK], F32, name="inv_sig2")
        nc.vector.reciprocal(out=inv_sig2[:], in_=sig2[:].rearrange("p a q -> p (a q)"))
        both_shape = [P, 2 * PASSES, W, PACK]
        dist_both = dist[:].rearrange("p a h i t -> p (a h) i t")
        dist2 = keep.tile(both_shape, F32, name="dist2")
        nc.vector.tensor_tensor(out=dist2[:], in0=dist_both, in1=dist_both, op=ALU.mult)
        scaled = keep.tile(both_shape, F32, name="scaled")
        nc.vector.tensor_tensor(
            out=scaled[:],
            in0=dist2[:],
            in1=inv_sig2[:].rearrange("p (q t) -> p q t", t=PACK).unsqueeze(2).to_broadcast(both_shape),
            op=ALU.mult,
        )
        gauss = keep.tile([P, 2, PASSES, W, PACK], F32, name="gauss")
        nc.scalar.activation(
            out=gauss[:].rearrange("p a h i t -> p (a h i t)"),
            in_=scaled[:].rearrange("p q i t -> p (q i t)"),
            func=ACT.Exp,
            scale=-1.0,
        )

        f_psum = fpsum.tile([P, PASSES, C, PACK], F32, name="f_psum")
        nc.tensor.matmul(
            f_psum[:].rearrange("p h c t -> p (h c t)"),
            lhsT=ident16[:],
            rhs=f_raw[:].rearrange("p h t c -> p h c t"),
            start=True,
            stop=True,
        )
        f_sbuf = keep.tile([P, PASSES, C, PACK], F32, name="f_sbuf")
        nc.scalar.copy(out=f_sbuf[:], in_=f_psum[:])
        spatial = keep.tile([P, PASSES, W, H, PACK], F32, name="spatial")
        for h in range(PASSES):
            nc.vector.tensor_tensor(
                out=spatial[:, h],
                in0=gauss[:, 0, h].unsqueeze(2).to_broadcast([P, W, H, PACK]),
                in1=gauss[:, 1, h].unsqueeze(1).to_broadcast([P, W, H, PACK]),
                op=ALU.mult,
            )

        go_bf = keep.tile([P, ROW_TILES, PASSES * P * PACK], BF16, name="go_bf", align_bytes=64)
        go_codes = keep.tile([P, ROW_TILES, PASSES, P], U32, name="go_codes", align_bytes=64)
        go_scales = keep.tile([P, ROW_TILES, PASSES, P], U8, name="go_scales", align_bytes=64)
        gb_bf = [keep.tile([P, O * PACK], BF16, name="gb_bf%d" % g, align_bytes=64) for g in range(PASSES)]
        gb_codes = keep.tile([P, PASSES, O], U32, name="gb_codes", align_bytes=64)
        gb_scales = keep.tile([P, PASSES, O], U8, name="gb_scales", align_bytes=64)
        w_codes = [keep.tile([P, PASSES, N], U32, name="w_codes%d" % n, align_bytes=64) for n in range(COL_TILES)]
        w_scales = [keep.tile([P, PASSES, N], U8, name="w_scales%d" % n, align_bytes=64) for n in range(COL_TILES)]
        x_codes = [keep.tile([P, PASSES, N], U32, name="x_codes%d" % n, align_bytes=64) for n in range(COL_TILES)]
        x_scales = [keep.tile([P, PASSES, N], U8, name="x_scales%d" % n, align_bytes=64) for n in range(COL_TILES)]
        sum_i = [keep.tile([P, CJ], F32, name="sum_i%d" % q) for q in range(ROW_TILES)]
        ey = keep.tile([P, PASSES, PACK, H], F32, name="ey")
        d_features = keep.tile([P, PASSES, PACK, C], F32, name="d_features")
        w_bf = {}
        x_bf = {}
        dw_bank = {}
        times_ey = {}

        def transpose_g(m):
            g, r = divmod(m, PACK)
            words = g_raw[g][:].bitcast(F32)
            bank = psum.tile([P, PASSES, 2, P], F32, name="go_bank%d" % m, tag="bank")
            for h in range(PASSES):
                first = (O * r + PASS * h) // 2
                for u in range(2):
                    nc.tensor.transpose(bank[:, h, u, :], words[:, first + u : first + PASS // 2 : 2], ident32[:])
            nc.scalar.copy(
                out=go_bf[:, m, :].bitcast(F32).rearrange("p (h b u) -> p h b u", h=PASSES, u=2),
                in_=bank[:].rearrange("p h u b -> p h b u"),
            )

        def quantise_go(first, count):
            tiles = slice(first, first + count)
            nc.vector.quantize_mx(
                out=go_codes[:, tiles].rearrange("p m h b -> p (m h b)").bitcast(E5M2),
                scales=go_scales[:, tiles].rearrange("p m h b -> p (m h b)"),
                in_=go_bf[:, tiles, :].rearrange("p m w -> p (m w)"),
            )

        def interleave_g(g, quarter, copy):
            h, half = divmod(quarter, 2)
            sizes = dict(r=PACK, h=PASSES, half=2, m=2, t=PACK)
            src = g_raw[g][:].rearrange("p (r h half pair m t) -> p h half pair t m r", **sizes)
            dst = gb_bf[g][:].rearrange("p (h t half pair m r) -> p h half pair t m r", **sizes)
            copy(out=dst[:, h, half], in_=src[:, h, half])

        def quantise_gb(g):
            nc.vector.quantize_mx(out=gb_codes[:, g, :].bitcast(E5M2), scales=gb_scales[:, g, :], in_=gb_bf[g][:])

        def build_w(n, h, channels, engine, f_src):
            shape = [P, len(channels), S, PACK]
            engine.tensor_tensor(
                out=w_bf[n, h][:, channels.start : channels.stop],
                in0=f_src[:, h, TILE_C * n + channels.start : TILE_C * n + channels.stop, :]
                .unsqueeze(2)
                .to_broadcast(shape),
                in1=spatial[:, h].rearrange("p i j t -> p (i j) t").unsqueeze(1).to_broadcast(shape),
                op=ALU.mult,
            )

        def build_w_gpsimd(n, h):
            w_bf[n, h] = stage.tile([P, TILE_C, S, PACK], BF16, name="w_bf%d%d" % (n, h), tag="w_gpsimd", align_bytes=64)
            build_w(n, h, range(GPSIMD_CHANNELS[n, h]), nc.gpsimd, f_sbuf)

        def build_w_vector(n, h):
            if (n, h) not in GPSIMD_CHANNELS:
                w_bf[n, h] = stage.tile([P, TILE_C, S, PACK], BF16, name="w_bf%d%d" % (n, h), align_bytes=64)
            build_w(n, h, range(GPSIMD_CHANNELS.get((n, h), 0), TILE_C), nc.vector, f_psum)

        def quantise_w(n, h):
            nc.vector.quantize_mx(
                out=w_codes[n][:, h, :].bitcast(E4M3),
                scales=w_scales[n][:, h, :],
                in_=w_bf[n, h][:].rearrange("p c s t -> p (c s t)"),
            )

        def interleave_x(n, g, i, copy):
            if n not in x_bf:
                x_bf[n] = stage.tile(
                    [P, PASSES, TILE_I, C, H, PACK], BF16, name="x_bf%d" % n, tag="x_bf", bufs=3, align_bytes=64
                )
            src = x_raw[g][:].rearrange("p (r c i half j) -> p i c half r j", r=PACK, i=W, half=2, j=H // 2)
            dst = x_bf[n][:, g, i].rearrange("p c (half j) r -> p c half r j", half=2)
            copy(out=dst, in_=src[:, TILE_I * n + i])

        def quantise_x(n):
            nc.vector.quantize_mx(
                out=x_codes[n][:].rearrange("p g w -> p (g w)").bitcast(E4M3),
                scales=x_scales[n][:].rearrange("p g w -> p (g w)"),
                in_=x_bf[n][:].rearrange("p g i c j r -> p (g i c j r)"),
            )

        def out_0_tile(n, m):
            bank = psum.tile([P, N], F32, name="dx_bank%d%d" % (n, m), tag="bank")
            for h in range(PASSES):
                nc.tensor.matmul_mx(
                    out=bank[:],
                    lhsT=go_codes[:, m, h, :].bitcast(E5M2),
                    lhsT_scale=go_scales[:, m, h, :],
                    rhs=w_codes[n][:, h, :].bitcast(E4M3),
                    rhs_scale=w_scales[n][:, h, :],
                    start=h == 0,
                    stop=h == PASSES - 1,
                )
            result = stage.tile([P, N], F32, name="result%d%d" % (n, m), tag="result", bufs=RESULT_BUFS)
            nc.scalar.copy(out=result[:], in_=bank[:])
            nc.sync.dma_start(out=out_0_tiles[m // PACK, m % PACK, :, N * n : N * (n + 1)], in_=result[:])

        def dweight_tile(n, q):
            dw_bank[n, q] = psum.tile([P, TILE_I, CJ], F32, name="dw_bank%d%d" % (n, q), tag="bank")
            cols = slice(P * q, P * (q + 1))
            for g in range(PASSES):
                nc.tensor.matmul_mx(
                    out=dw_bank[n, q][:].rearrange("p i w -> p (i w)"),
                    lhsT=gb_codes[:, g, cols].bitcast(E5M2),
                    lhsT_scale=gb_scales[:, g, cols],
                    rhs=x_codes[n][:, g, :].bitcast(E4M3),
                    rhs_scale=x_scales[n][:, g, :],
                    start=g == 0,
                    stop=g == PASSES - 1,
                )

        def add_row(n, q, i):
            h, t = divmod(q, PACK)
            row = TILE_I * n + i
            ex = gauss[:, 0, h, row, t : t + 1]
            if row == 0:
                nc.vector.tensor_scalar(out=sum_i[q][:], in0=dw_bank[n, q][:, i], scalar1=ex, scalar2=None, op0=ALU.mult)
            else:
                nc.vector.scalar_tensor_tensor(
                    out=sum_i[q][:], in0=dw_bank[n, q][:, i], scalar=ex, in1=sum_i[q][:], op0=ALU.mult, op1=ALU.add
                )

        def multiply_ey(q):
            engine = nc.vector if q == ROW_TILES - 1 else nc.gpsimd
            times_ey[q] = stage.tile([P, C, H], F32, name="times_ey%d" % q, tag="times_ey", bufs=REDUCE_LAG + 2)
            engine.tensor_tensor(
                out=times_ey[q][:],
                in0=sum_i[q][:].rearrange("p (c j) -> p c j", j=H),
                in1=ey[:, q // PACK, q % PACK, :].unsqueeze(1).to_broadcast([P, C, H]),
                op=ALU.mult,
            )

        def reduce_j(q):
            nc.vector.tensor_reduce(
                out=d_features[:, q // PACK, q % PACK, :], in_=times_ey[q][:], axis=mybir.AxisListType.X, op=ALU.add
            )

        build_w_gpsimd(1, 1)
        build_w_vector(0, 0)
        build_w_vector(1, 1)
        build_w_vector(0, 1)
        for quarter in range(4):
            transpose_g(2 * quarter)
            transpose_g(2 * quarter + 1)
            interleave_g(0, quarter, nc.scalar.copy)
        quantise_w(0, 0)
        quantise_w(0, 1)
        quantise_go(0, 2)
        quantise_go(2, 2)
        quantise_w(1, 1)

        out_0_todo = [(n, m) for n in range(COL_TILES) for m in range(ROW_TILES)]
        build_w_gpsimd(2, 0)
        build_w_vector(1, 0)
        build_w_vector(2, 0)
        for m in range(PACK - 1):
            out_0_tile(*out_0_todo.pop(0))
        for i in range(TILE_I):
            interleave_x(0, 0, i, nc.scalar.copy)
        out_0_tile(*out_0_todo.pop(0))
        quantise_go(PACK, PACK)
        quantise_w(1, 0)
        for quarter in range(4):
            interleave_g(1, quarter, nc.vector.tensor_copy)
        for i in range(TILE_I):
            interleave_x(0, 1, i, nc.vector.tensor_copy)
        quantise_gb(0)
        quantise_gb(1)
        quantise_x(0)
        quantise_w(2, 0)
        for m in range(PACK + ROW_TILES - OUT_0_HELD_BACK - 1):
            out_0_tile(*out_0_todo.pop(0))
        interleave_x(1, 0, 0, nc.scalar.copy)
        out_0_tile(*out_0_todo.pop(0))
        interleave_x(1, 0, 1, nc.scalar.copy)
        nc.scalar.copy(out=ey[:], in_=gauss[:, 1].rearrange("p h j t -> p h t j"))

        x_todo = [(n, g, i) for n in range(1, COL_TILES) for g in range(PASSES) for i in range(TILE_I)][TILE_I:]
        w_todo = [(2, 1), (3, 0), (3, 1)]
        last = COL_TILES - 1
        for n in range(COL_TILES):
            if n < last:
                build_w_gpsimd(*w_todo[n])
                build_w_vector(*w_todo[n])
            out_0_every = ROW_TILES // OUT_0_HELD_BACK if n == 0 else 2
            for q in range(ROW_TILES):
                dweight_tile(n, q)
                add_row(n, q, 0)
                if q > 0:
                    add_row(n, q - 1, 1)
                elif n > 0:
                    add_row(n - 1, ROW_TILES - 1, 1)
                if n == last and q > 0:
                    multiply_ey(q - 1)
                if n == last and q > REDUCE_LAG:
                    reduce_j(q - 1 - REDUCE_LAG)
                if q % 2 == 0 and x_todo:
                    interleave_x(*x_todo.pop(0), nc.scalar.copy)
                if n < last and q == QUANTISE_AT:
                    quantise_x(n + 1)
                    quantise_w(*w_todo[n])
                if (q + 1) % out_0_every == 0:
                    out_0_tile(*out_0_todo.pop(0))

        add_row(last, ROW_TILES - 1, 1)
        multiply_ey(ROW_TILES - 1)
        for q in range(ROW_TILES - 1 - REDUCE_LAG, ROW_TILES):
            reduce_j(q)
        for n, m in out_0_todo:
            out_0_tile(n, m)
        nc.sync.dma_start(
            out=out_1.rearrange(by_feature, p=P, t=PACK), in_=d_features[:].rearrange("p h t c -> p h (t c)")
        )
